import numpy as np
import ml_dtypes


def mxq(x, axis, fmt="e4m3"):
    dtype, down = {"e4m3": (ml_dtypes.float8_e4m3fn, 7), "e5m2": (ml_dtypes.float8_e5m2, 14)}[fmt]
    v = np.moveaxis(np.asarray(x, np.float32).astype(ml_dtypes.bfloat16).astype(np.float64), axis, -1)
    blocks = v.reshape(v.shape[:-1] + (-1, 32))
    amax = np.abs(blocks).max(-1, keepdims=True)
    byte = np.maximum(np.where(amax > 0, np.frexp(amax)[1] - 1 + 127, 0) - down, 1)
    scale = np.exp2(byte - 127.0)
    codes = (blocks / scale).astype(np.float32).astype(dtype).astype(np.float64)
    return np.moveaxis((codes * scale).reshape(v.shape), -1, axis)


WIDE = False


def mx_kscale(k):
    if not WIDE:
        return np.ones(k)
    levels = np.array([10, -10, 5, -5, 0])
    a = np.random.permutation(np.resize(levels, k // 512 * 4)).reshape(k // 512, 4)
    idx = np.arange(k)
    return np.exp2(a[idx // 512, idx % 128 // 32])


BF16 = ml_dtypes.bfloat16


def bf(x):
    return np.asarray(x, np.float32).astype(BF16)


def f64(x):
    return np.asarray(x).astype(np.float64)


B, N, D, R, Q = 4, 4096, 512, 8, 16


def setup_inputs():
    s = mx_kscale(D)
    return {"x": bf(np.random.standard_normal((B, N, D)) * s),
            "w0": bf(np.random.standard_normal((B, N, R))),
            "core1": bf(np.random.standard_normal((R, D, Q)) / np.sqrt(D * R) / s[None, :, None]),
            "core2": bf(np.random.standard_normal((Q, D, R)) / np.sqrt(D * Q) / s[None, :, None])}


def reference(x, w0, core1, core2):
    xq = mxq(f64(x), 2, "e4m3")
    c1 = mxq(f64(core1), 1, "e4m3").transpose(1, 0, 2).reshape(D, R * Q)
    c2 = mxq(f64(core2), 1, "e4m3").transpose(1, 0, 2).reshape(D, Q * R)
    m1 = (xq @ c1).reshape(B, N, R, Q)
    m2 = (xq @ c2).reshape(B, N, Q, R)
    w1 = (f64(w0)[..., :, None] * m1).sum(-2)
    w2 = (w1[..., :, None] * m2).sum(-2)
    return w2

@@ -1,0 +1,215 @@
+from contextlib import ExitStack
+
+import concourse.mybir as mybir
+from concourse.masks import make_identity
+
+F32 = mybir.dt.float32
+BF16 = mybir.dt.bfloat16
+U32 = mybir.dt.uint32
+U8 = mybir.dt.uint8
+FP8X4 = mybir.dt.float8_e4m3fn_x4
+MULT = mybir.AluOpType.mult
+ADD = mybir.AluOpType.add
+AX = mybir.AxisListType.X
+
+P = 128
+TOKENS = 4 * 4096
+D = 512
+R = 8
+Q = 16
+TILES = TOKENS // P
+QUAD = 4
+NQ = TILES // QUAD
+BATCH = 16
+QPB = BATCH // QUAD
+
+FLOPS = 2 * TOKENS * D * (R * Q + Q * R) + 2 * TOKENS * (R * Q + Q * R)
+
+
+def tile_linear_pa_t_kernel(tc, x, w0, core1, core2, out):
+    nc = tc.nc
+    xv = x.flatten_outer_dims().rearrange("(p t) d -> p t d", t=TILES)
+    w0v = w0.flatten_outer_dims().rearrange("(p t) r -> p t r", t=TILES)
+    ov = out.flatten_outer_dims().rearrange("(p t) r -> p t r", t=TILES)
+
+    with ExitStack() as ctx:
+        const = ctx.enter_context(tc.tile_pool(name="const", bufs=1))
+        xin = ctx.enter_context(tc.tile_pool(name="xin", bufs=1))
+        gp = ctx.enter_context(tc.tile_pool(name="gp", bufs=3))
+        cp = ctx.enter_context(tc.tile_pool(name="cp", bufs=3))
+        ep = ctx.enter_context(tc.tile_pool(name="ep", bufs=2))
+        xtp = ctx.enter_context(tc.psum_pool(name="xtp", bufs=4))
+        m1p = ctx.enter_context(tc.psum_pool(name="m1p", bufs=1))
+        m2p = ctx.enter_context(tc.psum_pool(name="m2p", bufs=2))
+        op = ctx.enter_context(tc.psum_pool(name="op", bufs=1))
+        ctx.enter_context(tc.manual_schedule())
+
+        c1raw = const.tile([P, 2, R, 2 * Q], BF16, name="c1raw")
+        c2raw = const.tile([P, 2, Q, 2 * R], BF16, name="c2raw")
+        for u in range(2):
+            nc.scalar.dma_start(
+                out=c1raw[:, u, :, :],
+                in_=core1[:, 256 * u : 256 * u + 256, :].rearrange("r (p e) q -> p r (e q)", e=2),
+            )
+            nc.scalar.dma_start(
+                out=c2raw[:, u, :, :],
+                in_=core2[:, 256 * u : 256 * u + 256, :].rearrange("q (p e) r -> p q (e r)", e=2),
+            )
+        w0_sb = const.tile([P, TILES, R], BF16, name="w0_sb")
+        nc.scalar.dma_start(out=w0_sb[:], in_=w0v)
+        xq = []
+        for i in range(NQ):
+            xt_in = xin.tile([P, QUAD, D], BF16, name="x%d" % i)
+            nc.sync.dma_start(out=xt_in[:], in_=xv[:, QUAD * i : QUAD * i + QUAD, :])
+            xq.append(xt_in)
+
+        ident = const.tile([P, P], F32, name="ident")
+        make_identity(nc, ident[:])
+
+        cg = const.tile([P, 2 * P, 4], BF16, name="cg", align_bytes=64)
+        for u in range(2):
+            nc.vector.tensor_copy(
+                out=cg[:, 0:P, 2 * u : 2 * u + 2].rearrange("p (q r) e -> p q r e", r=R),
+                in_=c1raw[:, u, :, :].rearrange("p r (e q) -> p q r e", e=2),
+            )
+            nc.vector.tensor_copy(
+                out=cg[:, P : 2 * P, 2 * u : 2 * u + 2].rearrange("p (q r) e -> p q r e", r=R),
+                in_=c2raw[:, u, :, :].rearrange("p q (e r) -> p q r e", e=2),
+            )
+        cc = const.tile([P, 2 * P], U32, name="cc", align_bytes=64)
+        cs = const.tile([P, 2 * P], U8, name="cs", align_bytes=64)
+        nc.vector.quantize_mx(
+            out=cc[:].bitcast(FP8X4), scales=cs[:], in_=cg[:].rearrange("p c t -> p (c t)")
+        )
+
+        out_sb = const.tile([P, TILES, R], F32, name="out_sb")
+
+        xts = {}
+        gs = {}
+        cods = {}
+        m1s = {}
+        m2s = {}
+        p2s = {}
+        os_ = {}
+        oTss = {}
+
+        def transpose_quad(i):
+            x32 = xq[i][:].bitcast(F32)
+            banks = []
+            for h in range(2):
+                xt = xtp.tile([P, 2, 2, P], F32, name="xt", tag="xt")
+                for a in range(2):
+                    for u in range(2):
+                        nc.tensor.transpose(
+                            xt[:, a, u, :], x32[:, 2 * h + a, u * P : (u + 1) * P], ident[:]
+                        )
+                banks.append(xt)
+            xts[i] = banks
+
+        def copy_quad(i):
+            g = gp.tile([P, QUAD, P, 4], BF16, name="g", tag="g", align_bytes=64)
+            g32 = g[:].bitcast(F32)
+            for h in range(2):
+                nc.scalar.copy(
+                    out=g32[:, 2 * h : 2 * h + 2, :, :],
+                    in_=xts[i][h][:].rearrange("p a u k -> p a k u"),
+                )
+            gs[i] = g
+
+        def quantise_quad(i):
+            cod = cp.tile([P, QUAD * P], U32, name="cod", tag="cod", align_bytes=64)
+            scl = cp.tile([P, QUAD * P], U8, name="scl", tag="scl", align_bytes=64)
+            nc.vector.quantize_mx(
+                out=cod[:].bitcast(FP8X4),
+                scales=scl[:],
+                in_=gs[i][:].rearrange("p a k t -> p (a k t)"),
+            )
+            cods[i] = (cod, scl)
+
+        def mx_quad(i):
+            cod, scl = cods[i]
+            m1 = m1p.tile([P, QUAD, P], F32, name="m1", tag="m1")
+            m2 = m2p.tile([P, QUAD, P], F32, name="m2", tag="m2")
+            for half, m in ((0, m1), (1, m2)):
+                for a in range(QUAD):
+                    nc.tensor.matmul_mx(
+                        out=m[:, a, :],
+                        lhsT=cod[:, a * P : (a + 1) * P].bitcast(FP8X4),
+                        lhsT_scale=scl[:, a * P : (a + 1) * P],
+                        rhs=cc[:, half * P : (half + 1) * P].bitcast(FP8X4),
+                        rhs_scale=cs[:, half * P : (half + 1) * P],
+                        start=True,
+                        stop=True,
+                    )
+            m1s[i] = m1
+            m2s[i] = m2
+
+        p1s = {}
+
+        def stage1_mul(i):
+            p1 = ep.tile([P, QUAD, Q, R], F32, name="p1", tag="p1")
+            nc.vector.tensor_tensor(
+                out=p1[:],
+                in0=m1s[i][:].rearrange("p a (q r) -> p a q r", r=R),
+                in1=w0_sb[:, QUAD * i : QUAD * i + QUAD, :].unsqueeze(2).to_broadcast([P, QUAD, Q, R]),
+                op=MULT,
+            )
+            p1s[i] = p1
+
+        def stage1_sum_stage2_mul(i):
+            w1 = ep.tile([P, QUAD, Q], F32, name="w1", tag="w1")
+            nc.vector.tensor_reduce(out=w1[:], in_=p1s[i][:], axis=AX, op=ADD)
+            b, j = divmod(i, QPB)
+            if j == 0:
+                p2s[b] = ep.tile([P, Q, BATCH, R], F32, name="p2", tag="p2")
+            nc.vector.tensor_tensor(
+                out=p2s[b][:, :, QUAD * j : QUAD * j + QUAD, :].rearrange("p q a r -> p a q r"),
+                in0=m2s[i][:].rearrange("p a (q r) -> p a q r", r=R),
+                in1=w1[:].unsqueeze(3).to_broadcast([P, QUAD, Q, R]),
+                op=MULT,
+            )
+
+        def sum_batch(b):
+            o = op.tile([P, 2, P], F32, name="o", tag="o")
+            for q in range(Q):
+                nc.tensor.matmul(
+                    out=o[:, 0, :],
+                    lhsT=p2s[b][:, q, :, :].rearrange("p a r -> p (a r)"),
+                    rhs=ident[:],
+                    start=(q == 0),
+                    stop=(q == Q - 1),
+                    is_transpose=True,
+                )
+            oTs = ep.tile([P, P], F32, name="oTs", tag="oTs")
+            nc.scalar.copy(out=oTs[:], in_=o[:, 0, :])
+            os_[b] = o
+            oTss[b] = oTs
+
+        def finish_batch(b):
+            o = os_[b]
+            nc.tensor.transpose(o[:, 1, :], oTss[b][:], ident[:])
+            dst = out_sb[:, BATCH * b : BATCH * b + BATCH, :]
+            nc.scalar.copy(out=dst.rearrange("p a r -> p (a r)"), in_=o[:, 1, :])
+            nc.sync.dma_start(out=ov[:, BATCH * b : BATCH * b + BATCH, :], in_=dst)
+
+        pending = []
+        for i in range(-3, NQ):
+            if i >= 0:
+                stage1_mul(i)
+            if 0 <= i + 1 < NQ:
+                mx_quad(i + 1)
+            if i >= 0:
+                stage1_sum_stage2_mul(i)
+            if i + 3 < NQ:
+                transpose_quad(i + 3)
+                copy_quad(i + 3)
+            for b in pending:
+                finish_batch(b)
+            pending = []
+            if 0 <= i + 2 < NQ:
+                quantise_quad(i + 2)
+            if i >= 0 and i % QPB == QPB - 1:
+                sum_batch(i // QPB)
+                pending.append(i // QPB)
+        for b in pending:
+            finish_batch(b)

@@ -35,11 +35,11 @@ def tile_linear_pa_t_kernel(tc, x, w0, core1, core2, out):
     with ExitStack() as ctx:
         const = ctx.enter_context(tc.tile_pool(name="const", bufs=1))
         xin = ctx.enter_context(tc.tile_pool(name="xin", bufs=1))
-        gp = ctx.enter_context(tc.tile_pool(name="gp", bufs=3))
-        cp = ctx.enter_context(tc.tile_pool(name="cp", bufs=3))
+        gp = ctx.enter_context(tc.tile_pool(name="gp", bufs=4))
+        cp = ctx.enter_context(tc.tile_pool(name="cp", bufs=4))
         ep = ctx.enter_context(tc.tile_pool(name="ep", bufs=2))
-        xtp = ctx.enter_context(tc.psum_pool(name="xtp", bufs=4))
-        m1p = ctx.enter_context(tc.psum_pool(name="m1p", bufs=1))
+        xtp = ctx.enter_context(tc.psum_pool(name="xtp", bufs=3))
+        m1p = ctx.enter_context(tc.psum_pool(name="m1p", bufs=2))
         m2p = ctx.enter_context(tc.psum_pool(name="m2p", bufs=2))
         op = ctx.enter_context(tc.psum_pool(name="op", bufs=1))
         ctx.enter_context(tc.manual_schedule())
@@ -126,23 +126,20 @@ def tile_linear_pa_t_kernel(tc, x, w0, core1, core2, out):
             )
             cods[i] = (cod, scl)
 
-        def mx_quad(i):
+        def mx_quad(i, half, pool, store):
             cod, scl = cods[i]
-            m1 = m1p.tile([P, QUAD, P], F32, name="m1", tag="m1")
-            m2 = m2p.tile([P, QUAD, P], F32, name="m2", tag="m2")
-            for half, m in ((0, m1), (1, m2)):
-                for a in range(QUAD):
-                    nc.tensor.matmul_mx(
-                        out=m[:, a, :],
-                        lhsT=cod[:, a * P : (a + 1) * P].bitcast(FP8X4),
-                        lhsT_scale=scl[:, a * P : (a + 1) * P],
-                        rhs=cc[:, half * P : (half + 1) * P].bitcast(FP8X4),
-                        rhs_scale=cs[:, half * P : (half + 1) * P],
-                        start=True,
-                        stop=True,
-                    )
-            m1s[i] = m1
-            m2s[i] = m2
+            m = pool.tile([P, QUAD, P], F32, name="m%d" % half, tag="m%d" % half)
+            for a in range(QUAD):
+                nc.tensor.matmul_mx(
+                    out=m[:, a, :],
+                    lhsT=cod[:, a * P : (a + 1) * P].bitcast(FP8X4),
+                    lhsT_scale=scl[:, a * P : (a + 1) * P],
+                    rhs=cc[:, half * P : (half + 1) * P].bitcast(FP8X4),
+                    rhs_scale=cs[:, half * P : (half + 1) * P],
+                    start=True,
+                    stop=True,
+                )
+            store[i] = m
 
         p1s = {}
 
@@ -156,22 +153,29 @@ def tile_linear_pa_t_kernel(tc, x, w0, core1, core2, out):
             )
             p1s[i] = p1
 
-        def stage1_sum_stage2_mul(i):
+        w1s = {}
+
+        def stage1_sum(i):
             w1 = ep.tile([P, QUAD, Q], F32, name="w1", tag="w1")
             nc.vector.tensor_reduce(out=w1[:], in_=p1s[i][:], axis=AX, op=ADD)
+            w1s[i] = w1
+
+        def stage2_mul(i):
             b, j = divmod(i, QPB)
             if j == 0:
                 p2s[b] = ep.tile([P, Q, BATCH, R], F32, name="p2", tag="p2")
             nc.vector.tensor_tensor(
                 out=p2s[b][:, :, QUAD * j : QUAD * j + QUAD, :].rearrange("p q a r -> p a q r"),
                 in0=m2s[i][:].rearrange("p a (q r) -> p a q r", r=R),
-                in1=w1[:].unsqueeze(3).to_broadcast([P, QUAD, Q, R]),
+                in1=w1s[i][:].unsqueeze(3).to_broadcast([P, QUAD, Q, R]),
                 op=MULT,
             )
 
-        def sum_batch(b):
-            o = op.tile([P, 2, P], F32, name="o", tag="o")
-            for q in range(Q):
+        def sum_batch(b, q0, q1):
+            if q0 == 0:
+                os_[b] = op.tile([P, 2, P], F32, name="o", tag="o")
+            o = os_[b]
+            for q in range(q0, q1):
                 nc.tensor.matmul(
                     out=o[:, 0, :],
                     lhsT=p2s[b][:, q, :, :].rearrange("p a r -> p (a r)"),
@@ -180,10 +184,10 @@ def tile_linear_pa_t_kernel(tc, x, w0, core1, core2, out):
                     stop=(q == Q - 1),
                     is_transpose=True,
                 )
-            oTs = ep.tile([P, P], F32, name="oTs", tag="oTs")
-            nc.scalar.copy(out=oTs[:], in_=o[:, 0, :])
-            os_[b] = o
-            oTss[b] = oTs
+            if q1 == Q:
+                oTs = ep.tile([P, P], F32, name="oTs", tag="oTs")
+                nc.scalar.copy(out=oTs[:], in_=o[:, 0, :])
+                oTss[b] = oTs
 
         def finish_batch(b):
             o = os_[b]
@@ -192,24 +196,30 @@ def tile_linear_pa_t_kernel(tc, x, w0, core1, core2, out):
             nc.scalar.copy(out=dst.rearrange("p a r -> p (a r)"), in_=o[:, 1, :])
             nc.sync.dma_start(out=ov[:, BATCH * b : BATCH * b + BATCH, :], in_=dst)
 
-        pending = []
-        for i in range(-3, NQ):
-            if i >= 0:
-                stage1_mul(i)
-            if 0 <= i + 1 < NQ:
-                mx_quad(i + 1)
-            if i >= 0:
-                stage1_sum_stage2_mul(i)
-            if i + 3 < NQ:
-                transpose_quad(i + 3)
-                copy_quad(i + 3)
-            for b in pending:
-                finish_batch(b)
-            pending = []
-            if 0 <= i + 2 < NQ:
-                quantise_quad(i + 2)
-            if i >= 0 and i % QPB == QPB - 1:
-                sum_batch(i // QPB)
-                pending.append(i // QPB)
-        for b in pending:
-            finish_batch(b)
+        def inside(k):
+            return 0 <= k < NQ
+
+        for s in range(-4, NQ + 4):
+            if inside(s + 4):
+                transpose_quad(s + 4)
+                copy_quad(s + 4)
+            b, part = divmod(s - 5, QPB)
+            if 0 <= b < TILES // BATCH:
+                if part == 0:
+                    sum_batch(b, 0, Q // 2)
+                elif part == 1:
+                    sum_batch(b, Q // 2, Q)
+                elif part == 2:
+                    finish_batch(b)
+            if inside(s):
+                stage1_mul(s)
+            if inside(s + 2):
+                mx_quad(s + 2, 0, m1p, m1s)
+            if inside(s - 1):
+                stage2_mul(s - 1)
+            if inside(s + 1):
+                mx_quad(s + 1, 1, m2p, m2s)
+            if inside(s):
+                stage1_sum(s)
+            if inside(s + 3):
+                quantise_quad(s + 3)

@@ -10,7 +10,6 @@ U8 = mybir.dt.uint8
 FP8X4 = mybir.dt.float8_e4m3fn_x4
 MULT = mybir.AluOpType.mult
 ADD = mybir.AluOpType.add
-AX = mybir.AxisListType.X
 
 P = 128
 TOKENS = 4 * 4096
@@ -20,8 +19,10 @@ Q = 16
 TILES = TOKENS // P
 QUAD = 4
 NQ = TILES // QUAD
+OCT = 8
+NB = TILES // OCT
 BATCH = 16
-QPB = BATCH // QUAD
+NO = TILES // BATCH
 
 FLOPS = 2 * TOKENS * D * (R * Q + Q * R) + 2 * TOKENS * (R * Q + Q * R)
 
@@ -35,9 +36,11 @@ def tile_linear_pa_t_kernel(tc, x, w0, core1, core2, out):
     with ExitStack() as ctx:
         const = ctx.enter_context(tc.tile_pool(name="const", bufs=1))
         xin = ctx.enter_context(tc.tile_pool(name="xin", bufs=1))
-        gp = ctx.enter_context(tc.tile_pool(name="gp", bufs=4))
-        cp = ctx.enter_context(tc.tile_pool(name="cp", bufs=4))
+        gp = ctx.enter_context(tc.tile_pool(name="gp", bufs=3))
+        cp = ctx.enter_context(tc.tile_pool(name="cp", bufs=5))
+        p1p = ctx.enter_context(tc.tile_pool(name="p1p", bufs=4))
         ep = ctx.enter_context(tc.tile_pool(name="ep", bufs=2))
+        h2p = ctx.enter_context(tc.tile_pool(name="h2p", bufs=1))
         xtp = ctx.enter_context(tc.psum_pool(name="xtp", bufs=3))
         m1p = ctx.enter_context(tc.psum_pool(name="m1p", bufs=2))
         m2p = ctx.enter_context(tc.psum_pool(name="m2p", bufs=2))
@@ -69,8 +72,8 @@ def tile_linear_pa_t_kernel(tc, x, w0, core1, core2, out):
         cg = const.tile([P, 2 * P, 4], BF16, name="cg", align_bytes=64)
         for u in range(2):
             nc.vector.tensor_copy(
-                out=cg[:, 0:P, 2 * u : 2 * u + 2].rearrange("p (q r) e -> p q r e", r=R),
-                in_=c1raw[:, u, :, :].rearrange("p r (e q) -> p q r e", e=2),
+                out=cg[:, 0:P, 2 * u : 2 * u + 2].rearrange("p (r q) e -> p r q e", q=Q),
+                in_=c1raw[:, u, :, :].rearrange("p r (e q) -> p r q e", e=2),
             )
             nc.vector.tensor_copy(
                 out=cg[:, P : 2 * P, 2 * u : 2 * u + 2].rearrange("p (q r) e -> p q r e", r=R),
@@ -84,97 +87,115 @@ def tile_linear_pa_t_kernel(tc, x, w0, core1, core2, out):
 
         out_sb = const.tile([P, TILES, R], F32, name="out_sb")
 
-        xts = {}
         gs = {}
         cods = {}
         m1s = {}
         m2s = {}
+        p1s = {}
+        h1s = {}
+        h2s = {}
+        w1s = {}
         p2s = {}
-        os_ = {}
+        obank = {}
         oTss = {}
 
-        def transpose_quad(i):
-            x32 = xq[i][:].bitcast(F32)
-            banks = []
-            for h in range(2):
-                xt = xtp.tile([P, 2, 2, P], F32, name="xt", tag="xt")
-                for a in range(2):
-                    for u in range(2):
-                        nc.tensor.transpose(
-                            xt[:, a, u, :], x32[:, 2 * h + a, u * P : (u + 1) * P], ident[:]
-                        )
-                banks.append(xt)
-            xts[i] = banks
+        def transpose_pair(j, h):
+            if h == 0:
+                gs[j] = gp.tile([P, OCT, P, 4], BF16, name="g", tag="g", align_bytes=64)
+            x32 = xq[2 * j + h // 2][:].bitcast(F32)
+            xt = xtp.tile([P, 2, 2, P], F32, name="xt", tag="xt")
+            for a in range(2):
+                for u in range(2):
+                    nc.tensor.transpose(
+                        xt[:, a, u, :], x32[:, 2 * (h % 2) + a, u * P : (u + 1) * P], ident[:]
+                    )
+            nc.scalar.copy(
+                out=gs[j][:].bitcast(F32)[:, 2 * h : 2 * h + 2, :, :],
+                in_=xt[:].rearrange("p a u k -> p a k u"),
+            )
 
-        def copy_quad(i):
-            g = gp.tile([P, QUAD, P, 4], BF16, name="g", tag="g", align_bytes=64)
-            g32 = g[:].bitcast(F32)
-            for h in range(2):
-                nc.scalar.copy(
-                    out=g32[:, 2 * h : 2 * h + 2, :, :],
-                    in_=xts[i][h][:].rearrange("p a u k -> p a k u"),
-                )
-            gs[i] = g
-
-        def quantise_quad(i):
-            cod = cp.tile([P, QUAD * P], U32, name="cod", tag="cod", align_bytes=64)
-            scl = cp.tile([P, QUAD * P], U8, name="scl", tag="scl", align_bytes=64)
+        def quantise(j):
+            cod = cp.tile([P, OCT * P], U32, name="cod", tag="cod", align_bytes=64)
+            scl = cp.tile([P, OCT * P], U8, name="scl", tag="scl", align_bytes=64)
             nc.vector.quantize_mx(
                 out=cod[:].bitcast(FP8X4),
                 scales=scl[:],
-                in_=gs[i][:].rearrange("p a k t -> p (a k t)"),
+                in_=gs[j][:].rearrange("p a k t -> p (a k t)"),
             )
-            cods[i] = (cod, scl)
+            cods[j] = (cod, scl)
 
-        def mx_quad(i, half, pool, store):
-            cod, scl = cods[i]
+        def mx_quad(k, half, pool, store):
+            cod, scl = cods[k // 2]
             m = pool.tile([P, QUAD, P], F32, name="m%d" % half, tag="m%d" % half)
             for a in range(QUAD):
+                c0 = (QUAD * (k % 2) + a) * P
                 nc.tensor.matmul_mx(
                     out=m[:, a, :],
-                    lhsT=cod[:, a * P : (a + 1) * P].bitcast(FP8X4),
-                    lhsT_scale=scl[:, a * P : (a + 1) * P],
+                    lhsT=cod[:, c0 : c0 + P].bitcast(FP8X4),
+                    lhsT_scale=scl[:, c0 : c0 + P],
                     rhs=cc[:, half * P : (half + 1) * P].bitcast(FP8X4),
                     rhs_scale=cs[:, half * P : (half + 1) * P],
                     start=True,
                     stop=True,
                 )
-            store[i] = m
+            store[k] = m
 
-        p1s = {}
-
-        def stage1_mul(i):
-            p1 = ep.tile([P, QUAD, Q, R], F32, name="p1", tag="p1")
+        def stage1_mul(k):
+            p1 = p1p.tile([P, R, QUAD, Q], F32, name="p1", tag="p1")
             nc.vector.tensor_tensor(
-                out=p1[:],
-                in0=m1s[i][:].rearrange("p a (q r) -> p a q r", r=R),
-                in1=w0_sb[:, QUAD * i : QUAD * i + QUAD, :].unsqueeze(2).to_broadcast([P, QUAD, Q, R]),
+                out=p1[:].rearrange("p r a q -> p a r q"),
+                in0=m1s[k][:].rearrange("p a (r q) -> p a r q", q=Q),
+                in1=w0_sb[:, QUAD * k : QUAD * k + QUAD, :].unsqueeze(3).to_broadcast([P, QUAD, R, Q]),
                 op=MULT,
             )
-            p1s[i] = p1
+            p1s[k] = p1
 
-        w1s = {}
+        def stage1_fold8to4(k):
+            j, h = divmod(k, 2)
+            if h == 0:
+                h1s[j] = ep.tile([P, 2, 4, QUAD * Q], F32, name="h1", tag="h1")
+            nc.gpsimd.tensor_tensor(
+                out=h1s[j][:, h, :, :].rearrange("p r c -> p (r c)"),
+                in0=p1s[k][:, 0:4, :, :].rearrange("p r a q -> p (r a q)"),
+                in1=p1s[k][:, 4:8, :, :].rearrange("p r a q -> p (r a q)"),
+                op=ADD,
+            )
 
-        def stage1_sum(i):
-            w1 = ep.tile([P, QUAD, Q], F32, name="w1", tag="w1")
-            nc.vector.tensor_reduce(out=w1[:], in_=p1s[i][:], axis=AX, op=ADD)
-            w1s[i] = w1
+        def stage1_fold4to2(j):
+            h2 = h2p.tile([P, 2, 2, QUAD * Q], F32, name="h2", tag="h2")
+            nc.gpsimd.tensor_tensor(
+                out=h2[:].rearrange("p h r c -> p h (r c)"),
+                in0=h1s[j][:, :, 0:2, :].rearrange("p h r c -> p h (r c)"),
+                in1=h1s[j][:, :, 2:4, :].rearrange("p h r c -> p h (r c)"),
+                op=ADD,
+            )
+            h2s[j] = h2
 
-        def stage2_mul(i):
-            b, j = divmod(i, QPB)
-            if j == 0:
+        def stage1_fold2to1(j):
+            w1 = ep.tile([P, 2, QUAD * Q], F32, name="w1", tag="w1")
+            nc.vector.tensor_tensor(
+                out=w1[:], in0=h2s[j][:, :, 0, :], in1=h2s[j][:, :, 1, :], op=ADD
+            )
+            w1s[j] = w1
+
+        def stage2_mul(k):
+            b, i = divmod(k, BATCH // QUAD)
+            if i == 0:
                 p2s[b] = ep.tile([P, Q, BATCH, R], F32, name="p2", tag="p2")
             nc.vector.tensor_tensor(
-                out=p2s[b][:, :, QUAD * j : QUAD * j + QUAD, :].rearrange("p q a r -> p a q r"),
-                in0=m2s[i][:].rearrange("p a (q r) -> p a q r", r=R),
-                in1=w1s[i][:].unsqueeze(3).to_broadcast([P, QUAD, Q, R]),
+                out=p2s[b][:, :, QUAD * i : QUAD * i + QUAD, :].rearrange("p q a r -> p a q r"),
+                in0=m2s[k][:].rearrange("p a (q r) -> p a q r", r=R),
+                in1=w1s[k // 2][:, k % 2, :]
+                .rearrange("p (a q) -> p a q", q=Q)
+                .unsqueeze(3)
+                .to_broadcast([P, QUAD, Q, R]),
                 op=MULT,
             )
 
         def sum_batch(b, q0, q1):
             if q0 == 0:
-                os_[b] = op.tile([P, 2, P], F32, name="o", tag="o")
-            o = os_[b]
+                obank[b] = op.tile([P, 2, P], F32, name="o", tag="o")
+            o = obank[b]
             for q in range(q0, q1):
                 nc.tensor.matmul(
                     out=o[:, 0, :],
@@ -190,36 +211,42 @@ def tile_linear_pa_t_kernel(tc, x, w0, core1, core2, out):
                 oTss[b] = oTs
 
         def finish_batch(b):
-            o = os_[b]
+            o = obank[b]
             nc.tensor.transpose(o[:, 1, :], oTss[b][:], ident[:])
             dst = out_sb[:, BATCH * b : BATCH * b + BATCH, :]
             nc.scalar.copy(out=dst.rearrange("p a r -> p (a r)"), in_=o[:, 1, :])
             nc.sync.dma_start(out=ov[:, BATCH * b : BATCH * b + BATCH, :], in_=dst)
 
-        def inside(k):
-            return 0 <= k < NQ
+        def inside(j):
+            return 0 <= j < NB
 
-        for s in range(-4, NQ + 4):
-            if inside(s + 4):
-                transpose_quad(s + 4)
-                copy_quad(s + 4)
-            b, part = divmod(s - 5, QPB)
-            if 0 <= b < TILES // BATCH:
-                if part == 0:
-                    sum_batch(b, 0, Q // 2)
-                elif part == 1:
-                    sum_batch(b, Q // 2, Q)
-                elif part == 2:
-                    finish_batch(b)
-            if inside(s):
-                stage1_mul(s)
-            if inside(s + 2):
-                mx_quad(s + 2, 0, m1p, m1s)
+        for s in range(-3, NB + 7):
+            if inside(s - 2):
+                stage1_fold2to1(s - 2)
             if inside(s - 1):
-                stage2_mul(s - 1)
-            if inside(s + 1):
-                mx_quad(s + 1, 1, m2p, m2s)
-            if inside(s):
-                stage1_sum(s)
+                stage1_fold4to2(s - 1)
+            if inside(s - 6) and (s - 6) % 2 == 0:
+                finish_batch((s - 6) // 2)
             if inside(s + 3):
-                quantise_quad(s + 3)
+                for h in range(3):
+                    transpose_pair(s + 3, h)
+            if inside(s - 4):
+                b, part = divmod(s - 4, 2)
+                sum_batch(b, part * (Q // 2), (part + 1) * (Q // 2))
+            if inside(s + 3):
+                transpose_pair(s + 3, 3)
+            if inside(s):
+                for k in (2 * s, 2 * s + 1):
+                    stage1_mul(k)
+                    stage1_fold8to4(k)
+            if inside(s - 2):
+                for k in (2 * s - 4, 2 * s - 3):
+                    stage2_mul(k)
+            if inside(s + 1):
+                for k in (2 * s + 2, 2 * s + 3):
+                    mx_quad(k, 0, m1p, m1s)
+            if inside(s - 1):
+                for k in (2 * s - 2, 2 * s - 1):
+                    mx_quad(k, 1, m2p, m2s)
+            if inside(s + 2):
+                quantise(s + 2)

@@ -49,41 +49,63 @@ def tile_linear_pa_t_kernel(tc, x, w0, core1, core2, out):
 
         c1raw = const.tile([P, 2, R, 2 * Q], BF16, name="c1raw")
         c2raw = const.tile([P, 2, Q, 2 * R], BF16, name="c2raw")
-        for u in range(2):
-            nc.scalar.dma_start(
-                out=c1raw[:, u, :, :],
-                in_=core1[:, 256 * u : 256 * u + 256, :].rearrange("r (p e) q -> p r (e q)", e=2),
-            )
-            nc.scalar.dma_start(
-                out=c2raw[:, u, :, :],
-                in_=core2[:, 256 * u : 256 * u + 256, :].rearrange("q (p e) r -> p q (e r)", e=2),
-            )
         w0_sb = const.tile([P, TILES, R], BF16, name="w0_sb")
-        nc.scalar.dma_start(out=w0_sb[:], in_=w0v)
         xq = []
-        for i in range(NQ):
+
+        def load_x(i):
             xt_in = xin.tile([P, QUAD, D], BF16, name="x%d" % i)
             nc.sync.dma_start(out=xt_in[:], in_=xv[:, QUAD * i : QUAD * i + QUAD, :])
             xq.append(xt_in)
 
+        for i in range(2):
+            load_x(i)
+        for u in range(2):
+            nc.sync.dma_start(
+                out=c1raw[:, u, :, :],
+                in_=core1[:, 256 * u : 256 * u + 256, :].rearrange("r (p e) q -> p r (e q)", e=2),
+            )
+        nc.sync.dma_start(out=w0_sb[:], in_=w0v)
+        for i in range(2, 8):
+            load_x(i)
+        for u in range(2):
+            nc.sync.dma_start(
+                out=c2raw[:, u, :, :],
+                in_=core2[:, 256 * u : 256 * u + 256, :].rearrange("q (p e) r -> p q (e r)", e=2),
+            )
+        for i in range(8, NQ):
+            load_x(i)
+
         ident = const.tile([P, P], F32, name="ident")
         make_identity(nc, ident[:])
 
-        cg = const.tile([P, 2 * P, 4], BF16, name="cg", align_bytes=64)
-        for u in range(2):
-            nc.vector.tensor_copy(
-                out=cg[:, 0:P, 2 * u : 2 * u + 2].rearrange("p (r q) e -> p r q e", q=Q),
-                in_=c1raw[:, u, :, :].rearrange("p r (e q) -> p r q e", e=2),
+        ccs = []
+
+        def prepare_core(grouped_views, raw_views, name):
+            cg = const.tile([P, P, 4], BF16, name="cg" + name, align_bytes=64)
+            for u in range(2):
+                nc.vector.tensor_copy(out=grouped_views(cg, u), in_=raw_views(u))
+            cc = const.tile([P, P], U32, name="cc" + name, align_bytes=64)
+            cs = const.tile([P, P], U8, name="cs" + name, align_bytes=64)
+            nc.vector.quantize_mx(
+                out=cc[:].bitcast(FP8X4), scales=cs[:], in_=cg[:].rearrange("p c t -> p (c t)")
             )
-            nc.vector.tensor_copy(
-                out=cg[:, P : 2 * P, 2 * u : 2 * u + 2].rearrange("p (q r) e -> p q r e", r=R),
-                in_=c2raw[:, u, :, :].rearrange("p q (e r) -> p q r e", e=2),
+            ccs.append((cc, cs))
+
+        def prepare_core1():
+            prepare_core(
+                lambda cg, u: cg[:, :, 2 * u : 2 * u + 2].rearrange("p (r q) e -> p r q e", q=Q),
+                lambda u: c1raw[:, u, :, :].rearrange("p r (e q) -> p r q e", e=2),
+                "1",
             )
-        cc = const.tile([P, 2 * P], U32, name="cc", align_bytes=64)
-        cs = const.tile([P, 2 * P], U8, name="cs", align_bytes=64)
-        nc.vector.quantize_mx(
-            out=cc[:].bitcast(FP8X4), scales=cs[:], in_=cg[:].rearrange("p c t -> p (c t)")
-        )
+
+        def prepare_core2():
+            prepare_core(
+                lambda cg, u: cg[:, :, 2 * u : 2 * u + 2].rearrange("p (q r) e -> p q r e", r=R),
+                lambda u: c2raw[:, u, :, :].rearrange("p q (e r) -> p q r e", e=2),
+                "2",
+            )
+
+        prepare_core1()
 
         out_sb = const.tile([P, TILES, R], F32, name="out_sb")
 
@@ -133,8 +155,8 @@ def tile_linear_pa_t_kernel(tc, x, w0, core1, core2, out):
                     out=m[:, a, :],
                     lhsT=cod[:, c0 : c0 + P].bitcast(FP8X4),
                     lhsT_scale=scl[:, c0 : c0 + P],
-                    rhs=cc[:, half * P : (half + 1) * P].bitcast(FP8X4),
-                    rhs_scale=cs[:, half * P : (half + 1) * P],
+                    rhs=ccs[half][0][:].bitcast(FP8X4),
+                    rhs_scale=ccs[half][1][:],
                     start=True,
                     stop=True,
                 )
@@ -220,33 +242,43 @@ def tile_linear_pa_t_kernel(tc, x, w0, core1, core2, out):
         def inside(j):
             return 0 <= j < NB
 
-        for s in range(-3, NB + 7):
+        q_parts = ((0, 6), (6, 11), (11, 16))
+
+        def output_work(s, half):
+            b, phase = divmod(2 * (s - 4) + half, 4)
+            if 0 <= b < NO:
+                if phase < 3:
+                    sum_batch(b, q_parts[phase][0], q_parts[phase][1])
+                else:
+                    finish_batch(b)
+
+        for s in range(-3, NB + 4):
             if inside(s - 2):
                 stage1_fold2to1(s - 2)
             if inside(s - 1):
                 stage1_fold4to2(s - 1)
-            if inside(s - 6) and (s - 6) % 2 == 0:
-                finish_batch((s - 6) // 2)
-            if inside(s + 3):
-                for h in range(3):
-                    transpose_pair(s + 3, h)
-            if inside(s - 4):
-                b, part = divmod(s - 4, 2)
-                sum_batch(b, part * (Q // 2), (part + 1) * (Q // 2))
-            if inside(s + 3):
-                transpose_pair(s + 3, 3)
             if inside(s):
                 for k in (2 * s, 2 * s + 1):
                     stage1_mul(k)
                     stage1_fold8to4(k)
-            if inside(s - 2):
-                for k in (2 * s - 4, 2 * s - 3):
-                    stage2_mul(k)
             if inside(s + 1):
                 for k in (2 * s + 2, 2 * s + 3):
                     mx_quad(k, 0, m1p, m1s)
+            if inside(s + 3):
+                transpose_pair(s + 3, 0)
+                transpose_pair(s + 3, 1)
+            output_work(s, 0)
+            if s == 1:
+                prepare_core2()
+            if inside(s - 2):
+                for k in (2 * s - 4, 2 * s - 3):
+                    stage2_mul(k)
             if inside(s - 1):
                 for k in (2 * s - 2, 2 * s - 1):
                     mx_quad(k, 1, m2p, m2s)
+            if inside(s + 3):
+                transpose_pair(s + 3, 2)
+                transpose_pair(s + 3, 3)
+            output_work(s, 1)
             if inside(s + 2):
                 quantise(s + 2)

@@ -37,10 +37,9 @@ def tile_linear_pa_t_kernel(tc, x, w0, core1, core2, out):
         const = ctx.enter_context(tc.tile_pool(name="const", bufs=1))
         xin = ctx.enter_context(tc.tile_pool(name="xin", bufs=1))
         gp = ctx.enter_context(tc.tile_pool(name="gp", bufs=3))
-        cp = ctx.enter_context(tc.tile_pool(name="cp", bufs=5))
+        cp = ctx.enter_context(tc.tile_pool(name="cp", bufs=3))
         p1p = ctx.enter_context(tc.tile_pool(name="p1p", bufs=4))
         ep = ctx.enter_context(tc.tile_pool(name="ep", bufs=2))
-        h2p = ctx.enter_context(tc.tile_pool(name="h2p", bufs=1))
         xtp = ctx.enter_context(tc.psum_pool(name="xtp", bufs=3))
         m1p = ctx.enter_context(tc.psum_pool(name="m1p", bufs=2))
         m2p = ctx.enter_context(tc.psum_pool(name="m2p", bufs=2))
@@ -49,63 +48,41 @@ def tile_linear_pa_t_kernel(tc, x, w0, core1, core2, out):
 
         c1raw = const.tile([P, 2, R, 2 * Q], BF16, name="c1raw")
         c2raw = const.tile([P, 2, Q, 2 * R], BF16, name="c2raw")
+        for u in range(2):
+            nc.scalar.dma_start(
+                out=c1raw[:, u, :, :],
+                in_=core1[:, 256 * u : 256 * u + 256, :].rearrange("r (p e) q -> p r (e q)", e=2),
+            )
+            nc.scalar.dma_start(
+                out=c2raw[:, u, :, :],
+                in_=core2[:, 256 * u : 256 * u + 256, :].rearrange("q (p e) r -> p q (e r)", e=2),
+            )
         w0_sb = const.tile([P, TILES, R], BF16, name="w0_sb")
+        nc.scalar.dma_start(out=w0_sb[:], in_=w0v)
         xq = []
-
-        def load_x(i):
+        for i in range(NQ):
             xt_in = xin.tile([P, QUAD, D], BF16, name="x%d" % i)
             nc.sync.dma_start(out=xt_in[:], in_=xv[:, QUAD * i : QUAD * i + QUAD, :])
             xq.append(xt_in)
 
-        for i in range(2):
-            load_x(i)
-        for u in range(2):
-            nc.sync.dma_start(
-                out=c1raw[:, u, :, :],
-                in_=core1[:, 256 * u : 256 * u + 256, :].rearrange("r (p e) q -> p r (e q)", e=2),
-            )
-        nc.sync.dma_start(out=w0_sb[:], in_=w0v)
-        for i in range(2, 8):
-            load_x(i)
-        for u in range(2):
-            nc.sync.dma_start(
-                out=c2raw[:, u, :, :],
-                in_=core2[:, 256 * u : 256 * u + 256, :].rearrange("q (p e) r -> p q (e r)", e=2),
-            )
-        for i in range(8, NQ):
-            load_x(i)
-
         ident = const.tile([P, P], F32, name="ident")
         make_identity(nc, ident[:])
 
-        ccs = []
-
-        def prepare_core(grouped_views, raw_views, name):
-            cg = const.tile([P, P, 4], BF16, name="cg" + name, align_bytes=64)
-            for u in range(2):
-                nc.vector.tensor_copy(out=grouped_views(cg, u), in_=raw_views(u))
-            cc = const.tile([P, P], U32, name="cc" + name, align_bytes=64)
-            cs = const.tile([P, P], U8, name="cs" + name, align_bytes=64)
-            nc.vector.quantize_mx(
-                out=cc[:].bitcast(FP8X4), scales=cs[:], in_=cg[:].rearrange("p c t -> p (c t)")
+        cg = const.tile([P, 2 * P, 4], BF16, name="cg", align_bytes=64)
+        for u in range(2):
+            nc.vector.tensor_copy(
+                out=cg[:, 0:P, 2 * u : 2 * u + 2].rearrange("p (r q) e -> p r q e", q=Q),
+                in_=c1raw[:, u, :, :].rearrange("p r (e q) -> p r q e", e=2),
             )
-            ccs.append((cc, cs))
-
-        def prepare_core1():
-            prepare_core(
-                lambda cg, u: cg[:, :, 2 * u : 2 * u + 2].rearrange("p (r q) e -> p r q e", q=Q),
-                lambda u: c1raw[:, u, :, :].rearrange("p r (e q) -> p r q e", e=2),
-                "1",
+            nc.vector.tensor_copy(
+                out=cg[:, P : 2 * P, 2 * u : 2 * u + 2].rearrange("p (q r) e -> p q r e", r=R),
+                in_=c2raw[:, u, :, :].rearrange("p q (e r) -> p q r e", e=2),
             )
-
-        def prepare_core2():
-            prepare_core(
-                lambda cg, u: cg[:, :, 2 * u : 2 * u + 2].rearrange("p (q r) e -> p q r e", r=R),
-                lambda u: c2raw[:, u, :, :].rearrange("p q (e r) -> p q r e", e=2),
-                "2",
-            )
-
-        prepare_core1()
+        cc = const.tile([P, 2 * P], U32, name="cc", align_bytes=64)
+        cs = const.tile([P, 2 * P], U8, name="cs", align_bytes=64)
+        nc.vector.quantize_mx(
+            out=cc[:].bitcast(FP8X4), scales=cs[:], in_=cg[:].rearrange("p c t -> p (c t)")
+        )
 
         out_sb = const.tile([P, TILES, R], F32, name="out_sb")
 
@@ -155,8 +132,8 @@ def tile_linear_pa_t_kernel(tc, x, w0, core1, core2, out):
                     out=m[:, a, :],
                     lhsT=cod[:, c0 : c0 + P].bitcast(FP8X4),
                     lhsT_scale=scl[:, c0 : c0 + P],
-                    rhs=ccs[half][0][:].bitcast(FP8X4),
-                    rhs_scale=ccs[half][1][:],
+                    rhs=cc[:, half * P : (half + 1) * P].bitcast(FP8X4),
+                    rhs_scale=cs[:, half * P : (half + 1) * P],
                     start=True,
                     stop=True,
                 )
@@ -184,7 +161,7 @@ def tile_linear_pa_t_kernel(tc, x, w0, core1, core2, out):
             )
 
         def stage1_fold4to2(j):
-            h2 = h2p.tile([P, 2, 2, QUAD * Q], F32, name="h2", tag="h2")
+            h2 = ep.tile([P, 2, 2, QUAD * Q], F32, name="h2", tag="h2")
             nc.gpsimd.tensor_tensor(
                 out=h2[:].rearrange("p h r c -> p h (r c)"),
                 in0=h1s[j][:, :, 0:2, :].rearrange("p h r c -> p h (r c)"),
@@ -242,43 +219,34 @@ def tile_linear_pa_t_kernel(tc, x, w0, core1, core2, out):
         def inside(j):
             return 0 <= j < NB
 
-        q_parts = ((0, 6), (6, 11), (11, 16))
-
-        def output_work(s, half):
-            b, phase = divmod(2 * (s - 4) + half, 4)
-            if 0 <= b < NO:
-                if phase < 3:
-                    sum_batch(b, q_parts[phase][0], q_parts[phase][1])
-                else:
-                    finish_batch(b)
-
         for s in range(-3, NB + 4):
-            if inside(s - 2):
-                stage1_fold2to1(s - 2)
-            if inside(s - 1):
-                stage1_fold4to2(s - 1)
             if inside(s):
-                for k in (2 * s, 2 * s + 1):
-                    stage1_mul(k)
-                    stage1_fold8to4(k)
+                stage1_fold4to2(s)
             if inside(s + 1):
+                quantise(s + 1)
                 for k in (2 * s + 2, 2 * s + 3):
                     mx_quad(k, 0, m1p, m1s)
-            if inside(s + 3):
-                transpose_pair(s + 3, 0)
-                transpose_pair(s + 3, 1)
-            output_work(s, 0)
-            if s == 1:
-                prepare_core2()
-            if inside(s - 2):
-                for k in (2 * s - 4, 2 * s - 3):
-                    stage2_mul(k)
             if inside(s - 1):
                 for k in (2 * s - 2, 2 * s - 1):
+                    stage2_mul(k)
+            if inside(s):
+                for k in (2 * s, 2 * s + 1):
                     mx_quad(k, 1, m2p, m2s)
+            if inside(s - 5) and (s - 5) % 2 == 0:
+                finish_batch((s - 5) // 2)
             if inside(s + 3):
-                transpose_pair(s + 3, 2)
+                for h in range(3):
+                    transpose_pair(s + 3, h)
+            if inside(s - 3):
+                b, part = divmod(s - 3, 2)
+                sum_batch(b, part * (Q // 2), (part + 1) * (Q // 2))
+            if inside(s + 3):
                 transpose_pair(s + 3, 3)
-            output_work(s, 1)
-            if inside(s + 2):
-                quantise(s + 2)
+            if inside(s + 1):
+                stage1_mul(2 * s + 2)
+                stage1_fold8to4(2 * s + 2)
+            if inside(s):
+                stage1_fold2to1(s)
+            if inside(s + 1):
+                stage1_mul(2 * s + 3)
+                stage1_fold8to4(2 * s + 3)

from contextlib import ExitStack

import concourse.mybir as mybir
from concourse.masks import make_identity

F32 = mybir.dt.float32
BF16 = mybir.dt.bfloat16
U32 = mybir.dt.uint32
U8 = mybir.dt.uint8
FP8X4 = mybir.dt.float8_e4m3fn_x4
MULT = mybir.AluOpType.mult
ADD = mybir.AluOpType.add

P = 128
TOKENS = 4 * 4096
D = 512
R = 8
Q = 16
TILES = TOKENS // P
QUAD = 4
NQ = TILES // QUAD
OCT = 8
NB = TILES // OCT
BATCH = 16
NO = TILES // BATCH

FLOPS = 2 * TOKENS * D * (R * Q + Q * R) + 2 * TOKENS * (R * Q + Q * R)


def tile_linear_pa_t_kernel(tc, x, w0, core1, core2, out):
    nc = tc.nc
    xv = x.flatten_outer_dims().rearrange("(p t) d -> p t d", t=TILES)
    w0v = w0.flatten_outer_dims().rearrange("(p t) r -> p t r", t=TILES)
    ov = out.flatten_outer_dims().rearrange("(p t) r -> p t r", t=TILES)

    with ExitStack() as ctx:
        const = ctx.enter_context(tc.tile_pool(name="const", bufs=1))
        xin = ctx.enter_context(tc.tile_pool(name="xin", bufs=1))
        gp = ctx.enter_context(tc.tile_pool(name="gp", bufs=3))
        cp = ctx.enter_context(tc.tile_pool(name="cp", bufs=3))
        p1p = ctx.enter_context(tc.tile_pool(name="p1p", bufs=4))
        ep = ctx.enter_context(tc.tile_pool(name="ep", bufs=2))
        xtp = ctx.enter_context(tc.psum_pool(name="xtp", bufs=3))
        m1p = ctx.enter_context(tc.psum_pool(name="m1p", bufs=2))
        m2p = ctx.enter_context(tc.psum_pool(name="m2p", bufs=2))
        op = ctx.enter_context(tc.psum_pool(name="op", bufs=1))
        ctx.enter_context(tc.manual_schedule())

        c1raw = const.tile([P, 2, R, 2 * Q], BF16, name="c1raw")
        c2raw = const.tile([P, 2, Q, 2 * R], BF16, name="c2raw")
        for u in range(2):
            nc.scalar.dma_start(
                out=c1raw[:, u, :, :],
                in_=core1[:, 256 * u : 256 * u + 256, :].rearrange("r (p e) q -> p r (e q)", e=2),
            )
            nc.scalar.dma_start(
                out=c2raw[:, u, :, :],
                in_=core2[:, 256 * u : 256 * u + 256, :].rearrange("q (p e) r -> p q (e r)", e=2),
            )
        w0_sb = const.tile([P, TILES, R], BF16, name="w0_sb")
        nc.scalar.dma_start(out=w0_sb[:], in_=w0v)
        xq = []
        for i in range(NQ):
            xt_in = xin.tile([P, QUAD, D], BF16, name="x%d" % i)
            nc.sync.dma_start(out=xt_in[:], in_=xv[:, QUAD * i : QUAD * i + QUAD, :])
            xq.append(xt_in)

        ident = const.tile([P, P], F32, name="ident")
        make_identity(nc, ident[:])

        cg = const.tile([P, 2 * P, 4], BF16, name="cg", align_bytes=64)
        for u in range(2):
            nc.vector.tensor_copy(
                out=cg[:, 0:P, 2 * u : 2 * u + 2].rearrange("p (r q) e -> p r q e", q=Q),
                in_=c1raw[:, u, :, :].rearrange("p r (e q) -> p r q e", e=2),
            )
            nc.vector.tensor_copy(
                out=cg[:, P : 2 * P, 2 * u : 2 * u + 2].rearrange("p (q r) e -> p q r e", r=R),
                in_=c2raw[:, u, :, :].rearrange("p q (e r) -> p q r e", e=2),
            )
        cc = const.tile([P, 2 * P], U32, name="cc", align_bytes=64)
        cs = const.tile([P, 2 * P], U8, name="cs", align_bytes=64)
        nc.vector.quantize_mx(
            out=cc[:].bitcast(FP8X4), scales=cs[:], in_=cg[:].rearrange("p c t -> p (c t)")
        )

        out_sb = const.tile([P, TILES, R], F32, name="out_sb")

        gs = {}
        cods = {}
        m1s = {}
        m2s = {}
        p1s = {}
        h1s = {}
        h2s = {}
        w1s = {}
        p2s = {}
        obank = {}
        oTss = {}

        def transpose_pair(j, h):
            if h == 0:
                gs[j] = gp.tile([P, OCT, P, 4], BF16, name="g", tag="g", align_bytes=64)
            x32 = xq[2 * j + h // 2][:].bitcast(F32)
            xt = xtp.tile([P, 2, 2, P], F32, name="xt", tag="xt")
            for a in range(2):
                for u in range(2):
                    nc.tensor.transpose(
                        xt[:, a, u, :], x32[:, 2 * (h % 2) + a, u * P : (u + 1) * P], ident[:]
                    )
            nc.scalar.copy(
                out=gs[j][:].bitcast(F32)[:, 2 * h : 2 * h + 2, :, :],
                in_=xt[:].rearrange("p a u k -> p a k u"),
            )

        def quantise(j):
            cod = cp.tile([P, OCT * P], U32, name="cod", tag="cod", align_bytes=64)
            scl = cp.tile([P, OCT * P], U8, name="scl", tag="scl", align_bytes=64)
            nc.vector.quantize_mx(
                out=cod[:].bitcast(FP8X4),
                scales=scl[:],
                in_=gs[j][:].rearrange("p a k t -> p (a k t)"),
            )
            cods[j] = (cod, scl)

        def mx_quad(k, half, pool, store):
            cod, scl = cods[k // 2]
            m = pool.tile([P, QUAD, P], F32, name="m%d" % half, tag="m%d" % half)
            for a in range(QUAD):
                c0 = (QUAD * (k % 2) + a) * P
                nc.tensor.matmul_mx(
                    out=m[:, a, :],
                    lhsT=cod[:, c0 : c0 + P].bitcast(FP8X4),
                    lhsT_scale=scl[:, c0 : c0 + P],
                    rhs=cc[:, half * P : (half + 1) * P].bitcast(FP8X4),
                    rhs_scale=cs[:, half * P : (half + 1) * P],
                    start=True,
                    stop=True,
                )
            store[k] = m

        def stage1_mul(k):
            p1 = p1p.tile([P, R, QUAD, Q], F32, name="p1", tag="p1")
            nc.vector.tensor_tensor(
                out=p1[:].rearrange("p r a q -> p a r q"),
                in0=m1s[k][:].rearrange("p a (r q) -> p a r q", q=Q),
                in1=w0_sb[:, QUAD * k : QUAD * k + QUAD, :].unsqueeze(3).to_broadcast([P, QUAD, R, Q]),
                op=MULT,
            )
            p1s[k] = p1

        def stage1_fold8to4(k):
            j, h = divmod(k, 2)
            if h == 0:
                h1s[j] = ep.tile([P, 2, 4, QUAD * Q], F32, name="h1", tag="h1")
            nc.gpsimd.tensor_tensor(
                out=h1s[j][:, h, :, :].rearrange("p r c -> p (r c)"),
                in0=p1s[k][:, 0:4, :, :].rearrange("p r a q -> p (r a q)"),
                in1=p1s[k][:, 4:8, :, :].rearrange("p r a q -> p (r a q)"),
                op=ADD,
            )

        def stage1_fold4to2(j):
            h2 = ep.tile([P, 2, 2, QUAD * Q], F32, name="h2", tag="h2")
            nc.gpsimd.tensor_tensor(
                out=h2[:].rearrange("p h r c -> p h (r c)"),
                in0=h1s[j][:, :, 0:2, :].rearrange("p h r c -> p h (r c)"),
                in1=h1s[j][:, :, 2:4, :].rearrange("p h r c -> p h (r c)"),
                op=ADD,
            )
            h2s[j] = h2

        def stage1_fold2to1(j):
            w1 = ep.tile([P, 2, QUAD * Q], F32, name="w1", tag="w1")
            nc.vector.tensor_tensor(
                out=w1[:], in0=h2s[j][:, :, 0, :], in1=h2s[j][:, :, 1, :], op=ADD
            )
            w1s[j] = w1

        def stage2_mul(k):
            b, i = divmod(k, BATCH // QUAD)
            if i == 0:
                p2s[b] = ep.tile([P, Q, BATCH, R], F32, name="p2", tag="p2")
            nc.vector.tensor_tensor(
                out=p2s[b][:, :, QUAD * i : QUAD * i + QUAD, :].rearrange("p q a r -> p a q r"),
                in0=m2s[k][:].rearrange("p a (q r) -> p a q r", r=R),
                in1=w1s[k // 2][:, k % 2, :]
                .rearrange("p (a q) -> p a q", q=Q)
                .unsqueeze(3)
                .to_broadcast([P, QUAD, Q, R]),
                op=MULT,
            )

        def sum_batch(b, q0, q1):
            if q0 == 0:
                obank[b] = op.tile([P, 2, P], F32, name="o", tag="o")
            o = obank[b]
            for q in range(q0, q1):
                nc.tensor.matmul(
                    out=o[:, 0, :],
                    lhsT=p2s[b][:, q, :, :].rearrange("p a r -> p (a r)"),
                    rhs=ident[:],
                    start=(q == 0),
                    stop=(q == Q - 1),
                    is_transpose=True,
                )
            if q1 == Q:
                oTs = ep.tile([P, P], F32, name="oTs", tag="oTs")
                nc.scalar.copy(out=oTs[:], in_=o[:, 0, :])
                oTss[b] = oTs

        def finish_batch(b):
            o = obank[b]
            nc.tensor.transpose(o[:, 1, :], oTss[b][:], ident[:])
            dst = out_sb[:, BATCH * b : BATCH * b + BATCH, :]
            nc.scalar.copy(out=dst.rearrange("p a r -> p (a r)"), in_=o[:, 1, :])
            nc.sync.dma_start(out=ov[:, BATCH * b : BATCH * b + BATCH, :], in_=dst)

        def inside(j):
            return 0 <= j < NB

        for s in range(-3, NB + 4):
            if inside(s):
                stage1_fold4to2(s)
            if inside(s + 1):
                quantise(s + 1)
                for k in (2 * s + 2, 2 * s + 3):
                    mx_quad(k, 0, m1p, m1s)
            if inside(s - 1):
                for k in (2 * s - 2, 2 * s - 1):
                    stage2_mul(k)
            if inside(s):
                for k in (2 * s, 2 * s + 1):
                    mx_quad(k, 1, m2p, m2s)
            if inside(s - 5) and (s - 5) % 2 == 0:
                finish_batch((s - 5) // 2)
            if inside(s + 3):
                for h in range(3):
                    transpose_pair(s + 3, h)
            if inside(s - 3):
                b, part = divmod(s - 3, 2)
                sum_batch(b, part * (Q // 2), (part + 1) * (Q // 2))
            if inside(s + 3):
                transpose_pair(s + 3, 3)
            if inside(s + 1):
                stage1_mul(2 * s + 2)
                stage1_fold8to4(2 * s + 2)
            if inside(s):
                stage1_fold2to1(s)
            if inside(s + 1):
                stage1_mul(2 * s + 3)
                stage1_fold8to4(2 * s + 3)
